import numpy as np
import ml_dtypes


def mxq(x, axis, fmt="e4m3"):
    dtype, down = {"e4m3": (ml_dtypes.float8_e4m3fn, 7), "e5m2": (ml_dtypes.float8_e5m2, 14)}[fmt]
    v = np.moveaxis(np.asarray(x, np.float32).astype(ml_dtypes.bfloat16).astype(np.float64), axis, -1)
    blocks = v.reshape(v.shape[:-1] + (-1, 32))
    amax = np.abs(blocks).max(-1, keepdims=True)
    byte = np.maximum(np.where(amax > 0, np.frexp(amax)[1] - 1 + 127, 0) - down, 1)
    scale = np.exp2(byte - 127.0)
    codes = (blocks / scale).astype(np.float32).astype(dtype).astype(np.float64)
    return np.moveaxis((codes * scale).reshape(v.shape), -1, axis)


WIDE = False


def mx_kscale(k):
    if not WIDE:
        return np.ones(k)
    levels = np.array([10, -10, 5, -5, 0])
    a = np.random.permutation(np.resize(levels, k // 512 * 4)).reshape(k // 512, 4)
    idx = np.arange(k)
    return np.exp2(a[idx // 512, idx % 128 // 32])


BF16 = ml_dtypes.bfloat16


def bf(x):
    return np.asarray(x, np.float32).astype(BF16)


def f64(x):
    return np.asarray(x).astype(np.float64)


S, E, C, HD, HP = 2048, 768, 256, 512, 8192
R = 2 * HP


def sigmoid(v):
    return 1.0 / (1.0 + np.exp(-v))


def setup_inputs():
    s, t = mx_kscale(R), mx_kscale(HD)
    return {"r": bf(np.abs(np.random.standard_normal((C, R))) * 0.5 * s),
            "psi_w1": bf(np.random.standard_normal((HD, R)) * 2.0 / np.sqrt(R) / s * t[:, None]),
            "psi_b1": bf(np.random.standard_normal(HD) * 0.3 * t),
            "w_dw": bf(np.random.standard_normal((E, HD)) * 1.5 / np.sqrt(HD) / t),
            "b_dw": bf(np.random.standard_normal(E) * 0.3),
            "w_gate": bf(np.random.standard_normal((E, HD)) * 1.5 / np.sqrt(HD) / t),
            "b_gate": bf(np.random.standard_normal(E) * 0.3),
            "W0": bf(np.random.standard_normal(E) * 0.1)}


def reference(r, psi_w1, psi_b1, w_dw, b_dw, w_gate, b_gate, W0):
    hid = np.maximum((mxq(f64(r), 1, "e4m3") @ mxq(f64(psi_w1), 1, "e4m3").T) + f64(psi_b1), 0.0)
    hq = mxq(hid, 1, "e4m3")
    dW = (hq @ mxq(f64(w_dw), 1, "e4m3").T) + f64(b_dw)
    gate = sigmoid((hq @ mxq(f64(w_gate), 1, "e4m3").T) + f64(b_gate))
    return f64(W0)[None, :] + gate * dW

@@ -1,0 +1,257 @@
+from contextlib import ExitStack
+
+import concourse.mybir as mybir
+from concourse.masks import make_identity
+
+F32 = mybir.dt.float32
+BF16 = mybir.dt.bfloat16
+U32 = mybir.dt.uint32
+U8 = mybir.dt.uint8
+FP8X4 = mybir.dt.float8_e4m3fn_x4
+ACT = mybir.ActivationFunctionType
+ALU = mybir.AluOpType
+
+P = 128
+PACK = 4
+K_PASS = P * PACK
+WORDS_PASS = K_PASS // 2
+
+CLASSES, R, HD, E = 256, 16384, 512, 768
+PASSES = R // K_PASS
+CLASS_SETS = CLASSES // P
+HD_SETS = HD // P
+ROW_SETS = CLASS_SETS + HD_SETS
+E_SETS = E // P
+E_PAIRS = E_SETS // 2
+
+CHUNK_PASSES = 4
+CHUNK_K = CHUNK_PASSES * K_PASS
+CHUNKS = PASSES // CHUNK_PASSES
+RAW_BUFS = 4
+RUN = 2
+ROUNDS = PASSES // RUN
+EDGE_PIECES = 4
+PREP_PASS = RAW_BUFS * CHUNK_PASSES
+
+FLOPS = 2 * CLASSES * R * HD + 2 * 2 * CLASSES * HD * E
+
+
+def tile_metalinearheadml_pb_k_kernel(tc, r, psi_w1, psi_b1, w_dw, b_dw, w_gate, b_gate, W0, out):
+    nc = tc.nc
+    with ExitStack() as stack:
+        consts = stack.enter_context(tc.tile_pool(name="consts", bufs=1))
+        raw_pool = stack.enter_context(tc.tile_pool(name="raw", bufs=RAW_BUFS))
+        grouped_pool = stack.enter_context(tc.tile_pool(name="grouped", bufs=2 * RUN))
+        codes_pool = stack.enter_context(tc.tile_pool(name="codes", bufs=3 * RUN))
+        tail_pool = stack.enter_context(tc.tile_pool(name="tail", bufs=E_SETS))
+        banks = stack.enter_context(tc.psum_pool(name="banks", bufs=4))
+        accs = stack.enter_context(tc.psum_pool(name="accs", bufs=1))
+        stack.enter_context(tc.manual_schedule())
+
+        ident = consts.tile([P, P], F32)
+        make_identity(nc, ident[:])
+        ones = consts.tile([P, P], BF16)
+        nc.vector.memset(ones[:], 1.0)
+        warm = consts.tile([P, 2], F32)
+        nc.vector.memset(warm[:], 0.0)
+        nc.scalar.activation(out=warm[:, 1:2], in_=warm[:, 0:1], func=ACT.Sigmoid)
+
+        r_rows = r.rearrange("(s p) k -> p s k", p=P)
+        w1_rows = psi_w1.rearrange("(u p e) k -> u p e k", u=2, e=2)
+
+        def load_chunk(c):
+            raw = raw_pool.tile([P, ROW_SETS, CHUNK_K], BF16)
+            pieces = EDGE_PIECES if c in (0, CHUNKS - 1) else 1
+            width = CHUNK_K // pieces
+            for piece in range(pieces):
+                cols = slice(piece * width, (piece + 1) * width)
+                k = slice(c * CHUNK_K + piece * width, c * CHUNK_K + (piece + 1) * width)
+                nc.sync.dma_start(out=raw[:, 0:CLASS_SETS, cols], in_=r_rows[:, :, k])
+                for u in range(2):
+                    first = CLASS_SETS + 2 * u
+                    nc.sync.dma_start(out=raw[:, first : first + 2, cols], in_=w1_rows[u][:, :, k])
+            return raw
+
+        raw_chunks = {}
+        for c in range(RAW_BUFS):
+            raw_chunks[c] = load_chunk(c)
+
+        w2_raw = consts.tile([P, 2 * E_SETS, HD], BF16)
+        nc.sync.dma_start(
+            out=w2_raw[:, 0:E_SETS, :].rearrange("p (v e) k -> p v (e k)", e=2),
+            in_=w_gate.rearrange("(v p e) k -> p v (e k)", p=P, e=2),
+        )
+        nc.sync.dma_start(
+            out=w2_raw[:, E_SETS : 2 * E_SETS, :].rearrange("p (v e) k -> p v (e k)", e=2),
+            in_=w_dw.rearrange("(v p e) k -> p v (e k)", p=P, e=2),
+        )
+        bias_rows = consts.tile([P, 2 * P], BF16)
+        nc.vector.memset(bias_rows[:], 0.0)
+        nc.scalar.dma_start(out=bias_rows[0:2, :], in_=psi_b1.rearrange("(v c) -> v c", c=2 * P))
+        nc.scalar.dma_start(out=bias_rows[2:5, :], in_=b_gate.rearrange("(v c) -> v c", c=2 * P))
+        nc.scalar.dma_start(out=bias_rows[5:8, :], in_=b_dw.rearrange("(v c) -> v c", c=2 * P))
+        w0_rows = consts.tile([P, E], BF16)
+        nc.vector.memset(w0_rows[:], 0.0)
+        nc.scalar.dma_start(out=w0_rows[0:1, :], in_=W0.rearrange("(o c) -> o c", o=1))
+        B1_COL, BGATE_COL, BDW_COL = 0, 4, 10
+
+        def transpose_pair(words, grouped, copy):
+            bank = banks.tile([P, 2, 2, P], F32, tag="bank")
+            for s in range(2):
+                for u in range(2):
+                    nc.tensor.transpose(bank[:, s, u, :], words[:, s, u * P : (u + 1) * P], ident[:])
+            copy(out=grouped.bitcast(F32), in_=bank[:].rearrange("p s u m -> p s m u"))
+
+        hid_acc = [accs.tile([P, CLASSES], F32, name="acc%d" % t, tag="acc%d" % t) for t in range(HD_SETS)]
+        grouped_of = {}
+        codes_of = {}
+
+        def transpose_pass(g):
+            words = raw_chunks[g // CHUNK_PASSES][:].bitcast(F32)
+            cols = slice((g % CHUNK_PASSES) * WORDS_PASS, (g % CHUNK_PASSES + 1) * WORDS_PASS)
+            r_grouped = grouped_pool.tile([P, CLASS_SETS, P, PACK], BF16, align_bytes=64)
+            w_grouped = grouped_pool.tile([P, HD_SETS, P, PACK], BF16, align_bytes=64)
+            transpose_pair(words[:, 0:2, cols], r_grouped[:], nc.vector.tensor_copy)
+            transpose_pair(words[:, 2:4, cols], w_grouped[:, 0:2], nc.scalar.copy)
+            transpose_pair(words[:, 4:6, cols], w_grouped[:, 2:4], nc.scalar.copy)
+            grouped_of[g] = (r_grouped, w_grouped)
+
+        def quantise_pass(g):
+            r_grouped, w_grouped = grouped_of[g]
+            r_codes = codes_pool.tile([P, CLASSES], U32, align_bytes=64)
+            r_scales = codes_pool.tile([P, CLASSES], U8, align_bytes=64)
+            w_codes = codes_pool.tile([P, HD], U32, align_bytes=64)
+            w_scales = codes_pool.tile([P, HD], U8, align_bytes=64)
+            nc.vector.quantize_mx(
+                out=r_codes[:].bitcast(FP8X4), scales=r_scales[:], in_=r_grouped[:].rearrange("p s m t -> p (s m t)")
+            )
+            nc.vector.quantize_mx(
+                out=w_codes[:].bitcast(FP8X4), scales=w_scales[:], in_=w_grouped[:].rearrange("p s m t -> p (s m t)")
+            )
+            codes_of[g] = (r_codes, r_scales, w_codes, w_scales)
+
+        def multiply_pass(g):
+            r_codes, r_scales, w_codes, w_scales = codes_of[g]
+            for t in range(HD_SETS):
+                units = slice(t * P, (t + 1) * P)
+                nc.tensor.matmul_mx(
+                    out=hid_acc[t][:],
+                    lhsT=w_codes[:, units].bitcast(FP8X4),
+                    lhsT_scale=w_scales[:, units],
+                    rhs=r_codes[:].bitcast(FP8X4),
+                    rhs_scale=r_scales[:],
+                    start=(g == 0),
+                    stop=(g == PASSES - 1),
+                )
+
+        w2_codes = consts.tile([P, 2 * E_SETS * P], U32, align_bytes=64)
+        w2_scales = consts.tile([P, 2 * E_SETS * P], U8, align_bytes=64)
+        w2_grouped_of = {}
+        bias_cols = consts.tile([P, 16], F32)
+        w0_all = consts.tile([P, E], F32)
+
+        def spread_small_operands():
+            bias_bank = banks.tile([P, 4 * P], F32, tag="bank")
+            nc.tensor.transpose(bias_bank[:, 0:P], bias_rows[:].bitcast(F32), ident[:])
+            nc.vector.tensor_copy(out=bias_cols[:], in_=bias_bank[:, 0:8].bitcast(BF16))
+            for first, width in ((0, 512), (512, 256)):
+                w0_bank = banks.tile([P, 4 * P], F32, tag="bank")
+                nc.tensor.matmul(
+                    out=w0_bank[:, 0:width], lhsT=ones[:], rhs=w0_rows[:, first : first + width], start=True, stop=True
+                )
+                nc.scalar.copy(out=w0_all[:, first : first + width], in_=w0_bank[:, 0:width])
+
+        def transpose_w2_pair(pair):
+            w2_grouped = grouped_pool.tile([P, 2, P, PACK], BF16, align_bytes=64)
+            transpose_pair(w2_raw[:].bitcast(F32)[:, 2 * pair : 2 * pair + 2, :], w2_grouped[:], nc.scalar.copy)
+            w2_grouped_of[pair] = w2_grouped
+
+        def quantise_w2_pair(pair):
+            cols = slice(2 * pair * P, (2 * pair + 2) * P)
+            nc.vector.quantize_mx(
+                out=w2_codes[:, cols].bitcast(FP8X4),
+                scales=w2_scales[:, cols],
+                in_=w2_grouped_of[pair][:].rearrange("p s m t -> p (s m t)"),
+            )
+
+        for i in range(ROUNDS + 2):
+            for g in range(i * RUN, (i + 1) * RUN):
+                if g < PASSES:
+                    transpose_pass(g)
+                    last_of_chunk = g % CHUNK_PASSES == CHUNK_PASSES - 1
+                    if last_of_chunk and g // CHUNK_PASSES + RAW_BUFS < CHUNKS:
+                        raw_chunks[g // CHUNK_PASSES + RAW_BUFS] = load_chunk(g // CHUNK_PASSES + RAW_BUFS)
+                if g == 0:
+                    spread_small_operands()
+                if 0 <= g - PREP_PASS < E_SETS:
+                    transpose_w2_pair(g - PREP_PASS)
+                if 0 <= g - RUN < PASSES:
+                    quantise_pass(g - RUN)
+                if 0 <= g - RUN - PREP_PASS < E_SETS:
+                    quantise_w2_pair(g - RUN - PREP_PASS)
+            for g in range((i - 2) * RUN, (i - 1) * RUN):
+                if 0 <= g:
+                    multiply_pass(g)
+
+        hid_planes = consts.tile([P, HD_SETS, CLASSES], BF16)
+        for t in range(HD_SETS):
+            bias = bias_cols[:, B1_COL + t : B1_COL + t + 1]
+            if t % 2 == 0:
+                nc.scalar.activation(out=hid_planes[:, t, :], in_=hid_acc[t][:], func=ACT.Relu, bias=bias, scale=1.0)
+            else:
+                nc.vector.tensor_scalar(
+                    out=hid_planes[:, t, :], in0=hid_acc[t][:], scalar1=bias, scalar2=0.0, op0=ALU.add, op1=ALU.max
+                )
+        hid_grouped = consts.tile([P, CLASSES, PACK], BF16, align_bytes=64)
+        nc.vector.tensor_copy(out=hid_grouped[:], in_=hid_planes[:].rearrange("p t c -> p c t"))
+        hid_codes = consts.tile([P, CLASSES], U32, align_bytes=64)
+        hid_scales = consts.tile([P, CLASSES], U8, align_bytes=64)
+        nc.vector.quantize_mx(
+            out=hid_codes[:].bitcast(FP8X4), scales=hid_scales[:], in_=hid_grouped[:].rearrange("p c t -> p (c t)")
+        )
+
+        products = []
+        for j in range(E_SETS):
+            pre = banks.tile([P, 2, CLASSES], F32, tag="bank")
+            for plane in range(2):
+                outputs = slice((plane * E_SETS + j) * P, (plane * E_SETS + j + 1) * P)
+                nc.tensor.matmul_mx(
+                    out=pre[:, plane, :],
+                    lhsT=w2_codes[:, outputs].bitcast(FP8X4),
+                    lhsT_scale=w2_scales[:, outputs],
+                    rhs=hid_codes[:].bitcast(FP8X4),
+                    rhs_scale=hid_scales[:],
+                    start=True,
+                    stop=True,
+                )
+            gate = tail_pool.tile([P, CLASSES], F32)
+            nc.scalar.activation(
+                out=gate[:], in_=pre[:, 0, :], func=ACT.Sigmoid, bias=bias_cols[:, BGATE_COL + j : BGATE_COL + j + 1], scale=1.0
+            )
+            product = tail_pool.tile([P, CLASSES], F32)
+            nc.vector.scalar_tensor_tensor(
+                out=product[:],
+                in0=pre[:, 1, :],
+                scalar=bias_cols[:, BDW_COL + j : BDW_COL + j + 1],
+                in1=gate[:],
+                op0=ALU.add,
+                op1=ALU.mult,
+            )
+            products.append(product)
+
+        out_rows = out.rearrange("(c p) x -> p c x", p=P)
+        for v in range(E_PAIRS):
+            back = accs.tile([P, CLASS_SETS, 2, P], F32, name="back%d" % v, tag="acc%d" % v)
+            for e in range(2):
+                for c in range(CLASS_SETS):
+                    nc.tensor.transpose(back[:, c, e, :], products[2 * v + e][:, c * P : (c + 1) * P], ident[:])
+            result = tail_pool.tile([P, CLASS_SETS, 2 * P], F32, bufs=E_PAIRS)
+            outputs = slice(v * 2 * P, (v + 1) * 2 * P)
+            w0_pairs = w0_all[:, outputs].rearrange("p (m e) -> p m e", e=2)
+            nc.vector.tensor_tensor(
+                out=result[:].rearrange("p c (m e) -> p c m e", e=2),
+                in0=back[:].rearrange("p c e m -> p c m e"),
+                in1=w0_pairs.unsqueeze(1).to_broadcast([P, CLASS_SETS, P, 2]),
+                op=ALU.add,
+            )
+            nc.sync.dma_start(out=out_rows[:, :, outputs], in_=result[:])

@@ -28,7 +28,7 @@ CHUNK_PASSES = 4
 CHUNK_K = CHUNK_PASSES * K_PASS
 CHUNKS = PASSES // CHUNK_PASSES
 RAW_BUFS = 4
-RUN = 2
+RUN = 1
 ROUNDS = PASSES // RUN
 EDGE_PIECES = 4
 PREP_PASS = RAW_BUFS * CHUNK_PASSES
@@ -41,8 +41,8 @@ def tile_metalinearheadml_pb_k_kernel(tc, r, psi_w1, psi_b1, w_dw, b_dw, w_gate,
     with ExitStack() as stack:
         consts = stack.enter_context(tc.tile_pool(name="consts", bufs=1))
         raw_pool = stack.enter_context(tc.tile_pool(name="raw", bufs=RAW_BUFS))
-        grouped_pool = stack.enter_context(tc.tile_pool(name="grouped", bufs=2 * RUN))
-        codes_pool = stack.enter_context(tc.tile_pool(name="codes", bufs=3 * RUN))
+        grouped_pool = stack.enter_context(tc.tile_pool(name="grouped", bufs=2 * RUN + 2))
+        codes_pool = stack.enter_context(tc.tile_pool(name="codes", bufs=3 * RUN + 2))
         tail_pool = stack.enter_context(tc.tile_pool(name="tail", bufs=E_SETS))
         banks = stack.enter_context(tc.psum_pool(name="banks", bufs=4))
         accs = stack.enter_context(tc.psum_pool(name="accs", bufs=1))

@@ -111,7 +111,7 @@ def tile_metalinearheadml_pb_k_kernel(tc, r, psi_w1, psi_b1, w_dw, b_dw, w_gate,
             cols = slice((g % CHUNK_PASSES) * WORDS_PASS, (g % CHUNK_PASSES + 1) * WORDS_PASS)
             r_grouped = grouped_pool.tile([P, CLASS_SETS, P, PACK], BF16, align_bytes=64)
             w_grouped = grouped_pool.tile([P, HD_SETS, P, PACK], BF16, align_bytes=64)
-            transpose_pair(words[:, 0:2, cols], r_grouped[:], nc.vector.tensor_copy)
+            transpose_pair(words[:, 0:2, cols], r_grouped[:], nc.vector.tensor_copy if g % 2 == 0 else nc.scalar.copy)
             transpose_pair(words[:, 2:4, cols], w_grouped[:, 0:2], nc.scalar.copy)
             transpose_pair(words[:, 4:6, cols], w_grouped[:, 2:4], nc.scalar.copy)
             grouped_of[g] = (r_grouped, w_grouped)
@@ -161,9 +161,9 @@ def tile_metalinearheadml_pb_k_kernel(tc, r, psi_w1, psi_b1, w_dw, b_dw, w_gate,
                 )
                 nc.scalar.copy(out=w0_all[:, first : first + width], in_=w0_bank[:, 0:width])
 
-        def transpose_w2_pair(pair):
+        def transpose_w2_pair(pair, copy):
             w2_grouped = grouped_pool.tile([P, 2, P, PACK], BF16, align_bytes=64)
-            transpose_pair(w2_raw[:].bitcast(F32)[:, 2 * pair : 2 * pair + 2, :], w2_grouped[:], nc.scalar.copy)
+            transpose_pair(w2_raw[:].bitcast(F32)[:, 2 * pair : 2 * pair + 2, :], w2_grouped[:], copy)
             w2_grouped_of[pair] = w2_grouped
 
         def quantise_w2_pair(pair):
@@ -184,7 +184,7 @@ def tile_metalinearheadml_pb_k_kernel(tc, r, psi_w1, psi_b1, w_dw, b_dw, w_gate,
                 if g == 0:
                     spread_small_operands()
                 if 0 <= g - PREP_PASS < E_SETS:
-                    transpose_w2_pair(g - PREP_PASS)
+                    transpose_w2_pair(g - PREP_PASS, nc.scalar.copy if g % 2 == 0 else nc.vector.tensor_copy)
                 if 0 <= g - RUN < PASSES:
                     quantise_pass(g - RUN)
                 if 0 <= g - RUN - PREP_PASS < E_SETS:

@@ -24,13 +24,12 @@ ROW_SETS = CLASS_SETS + HD_SETS
 E_SETS = E // P
 E_PAIRS = E_SETS // 2
 
-CHUNK_PASSES = 4
+CHUNK_PASSES = 2
 CHUNK_K = CHUNK_PASSES * K_PASS
 CHUNKS = PASSES // CHUNK_PASSES
-RAW_BUFS = 4
+RAW_BUFS = 8
 RUN = 1
 ROUNDS = PASSES // RUN
-EDGE_PIECES = 4
 PREP_PASS = RAW_BUFS * CHUNK_PASSES
 
 FLOPS = 2 * CLASSES * R * HD + 2 * 2 * CLASSES * HD * E
@@ -52,6 +51,15 @@ def tile_metalinearheadml_pb_k_kernel(tc, r, psi_w1, psi_b1, w_dw, b_dw, w_gate,
         make_identity(nc, ident[:])
         ones = consts.tile([P, P], BF16)
         nc.vector.memset(ones[:], 1.0)
+
+        bias_rows = consts.tile([P, 2 * P], BF16)
+        nc.vector.memset(bias_rows[:], 0.0)
+        nc.scalar.dma_start(out=bias_rows[0:2, :], in_=psi_b1.rearrange("(v c) -> v c", c=2 * P))
+        nc.scalar.dma_start(out=bias_rows[2:5, :], in_=b_gate.rearrange("(v c) -> v c", c=2 * P))
+        nc.scalar.dma_start(out=bias_rows[5:8, :], in_=b_dw.rearrange("(v c) -> v c", c=2 * P))
+        w0_rows = consts.tile([P, E], BF16)
+        nc.vector.memset(w0_rows[:], 0.0)
+        nc.scalar.dma_start(out=w0_rows[0:1, :], in_=W0.rearrange("(o c) -> o c", o=1))
         warm = consts.tile([P, 2], F32)
         nc.vector.memset(warm[:], 0.0)
         nc.scalar.activation(out=warm[:, 1:2], in_=warm[:, 0:1], func=ACT.Sigmoid)
@@ -61,15 +69,11 @@ def tile_metalinearheadml_pb_k_kernel(tc, r, psi_w1, psi_b1, w_dw, b_dw, w_gate,
 
         def load_chunk(c):
             raw = raw_pool.tile([P, ROW_SETS, CHUNK_K], BF16)
-            pieces = EDGE_PIECES if c in (0, CHUNKS - 1) else 1
-            width = CHUNK_K // pieces
-            for piece in range(pieces):
-                cols = slice(piece * width, (piece + 1) * width)
-                k = slice(c * CHUNK_K + piece * width, c * CHUNK_K + (piece + 1) * width)
-                nc.sync.dma_start(out=raw[:, 0:CLASS_SETS, cols], in_=r_rows[:, :, k])
-                for u in range(2):
-                    first = CLASS_SETS + 2 * u
-                    nc.sync.dma_start(out=raw[:, first : first + 2, cols], in_=w1_rows[u][:, :, k])
+            k = slice(c * CHUNK_K, (c + 1) * CHUNK_K)
+            nc.sync.dma_start(out=raw[:, 0:CLASS_SETS, :], in_=r_rows[:, :, k])
+            for u in range(2):
+                first = CLASS_SETS + 2 * u
+                nc.sync.dma_start(out=raw[:, first : first + 2, :], in_=w1_rows[u][:, :, k])
             return raw
 
         raw_chunks = {}
@@ -85,14 +89,6 @@ def tile_metalinearheadml_pb_k_kernel(tc, r, psi_w1, psi_b1, w_dw, b_dw, w_gate,
             out=w2_raw[:, E_SETS : 2 * E_SETS, :].rearrange("p (v e) k -> p v (e k)", e=2),
             in_=w_dw.rearrange("(v p e) k -> p v (e k)", p=P, e=2),
         )
-        bias_rows = consts.tile([P, 2 * P], BF16)
-        nc.vector.memset(bias_rows[:], 0.0)
-        nc.scalar.dma_start(out=bias_rows[0:2, :], in_=psi_b1.rearrange("(v c) -> v c", c=2 * P))
-        nc.scalar.dma_start(out=bias_rows[2:5, :], in_=b_gate.rearrange("(v c) -> v c", c=2 * P))
-        nc.scalar.dma_start(out=bias_rows[5:8, :], in_=b_dw.rearrange("(v c) -> v c", c=2 * P))
-        w0_rows = consts.tile([P, E], BF16)
-        nc.vector.memset(w0_rows[:], 0.0)
-        nc.scalar.dma_start(out=w0_rows[0:1, :], in_=W0.rearrange("(o c) -> o c", o=1))
         B1_COL, BGATE_COL, BDW_COL = 0, 4, 10
 
         def transpose_pair(words, grouped, copy):
@@ -111,7 +107,7 @@ def tile_metalinearheadml_pb_k_kernel(tc, r, psi_w1, psi_b1, w_dw, b_dw, w_gate,
             cols = slice((g % CHUNK_PASSES) * WORDS_PASS, (g % CHUNK_PASSES + 1) * WORDS_PASS)
             r_grouped = grouped_pool.tile([P, CLASS_SETS, P, PACK], BF16, align_bytes=64)
             w_grouped = grouped_pool.tile([P, HD_SETS, P, PACK], BF16, align_bytes=64)
-            transpose_pair(words[:, 0:2, cols], r_grouped[:], nc.vector.tensor_copy if g % 2 == 0 else nc.scalar.copy)
+            transpose_pair(words[:, 0:2, cols], r_grouped[:], nc.vector.tensor_copy)
             transpose_pair(words[:, 2:4, cols], w_grouped[:, 0:2], nc.scalar.copy)
             transpose_pair(words[:, 4:6, cols], w_grouped[:, 2:4], nc.scalar.copy)
             grouped_of[g] = (r_grouped, w_grouped)
@@ -161,9 +157,9 @@ def tile_metalinearheadml_pb_k_kernel(tc, r, psi_w1, psi_b1, w_dw, b_dw, w_gate,
                 )
                 nc.scalar.copy(out=w0_all[:, first : first + width], in_=w0_bank[:, 0:width])
 
-        def transpose_w2_pair(pair, copy):
+        def transpose_w2_pair(pair):
             w2_grouped = grouped_pool.tile([P, 2, P, PACK], BF16, align_bytes=64)
-            transpose_pair(w2_raw[:].bitcast(F32)[:, 2 * pair : 2 * pair + 2, :], w2_grouped[:], copy)
+            transpose_pair(w2_raw[:].bitcast(F32)[:, 2 * pair : 2 * pair + 2, :], w2_grouped[:], nc.scalar.copy)
             w2_grouped_of[pair] = w2_grouped
 
         def quantise_w2_pair(pair):
@@ -181,10 +177,10 @@ def tile_metalinearheadml_pb_k_kernel(tc, r, psi_w1, psi_b1, w_dw, b_dw, w_gate,
                     last_of_chunk = g % CHUNK_PASSES == CHUNK_PASSES - 1
                     if last_of_chunk and g // CHUNK_PASSES + RAW_BUFS < CHUNKS:
                         raw_chunks[g // CHUNK_PASSES + RAW_BUFS] = load_chunk(g // CHUNK_PASSES + RAW_BUFS)
-                if g == 0:
+                if g == CHUNK_PASSES - 1:
                     spread_small_operands()
                 if 0 <= g - PREP_PASS < E_SETS:
-                    transpose_w2_pair(g - PREP_PASS, nc.scalar.copy if g % 2 == 0 else nc.vector.tensor_copy)
+                    transpose_w2_pair(g - PREP_PASS)
                 if 0 <= g - RUN < PASSES:
                     quantise_pass(g - RUN)
                 if 0 <= g - RUN - PREP_PASS < E_SETS:

@@ -45,7 +45,6 @@ def tile_metalinearheadml_pb_k_kernel(tc, r, psi_w1, psi_b1, w_dw, b_dw, w_gate,
         tail_pool = stack.enter_context(tc.tile_pool(name="tail", bufs=E_SETS))
         banks = stack.enter_context(tc.psum_pool(name="banks", bufs=4))
         accs = stack.enter_context(tc.psum_pool(name="accs", bufs=1))
-        stack.enter_context(tc.manual_schedule())
 
         ident = consts.tile([P, P], F32)
         make_identity(nc, ident[:])

@@ -45,6 +45,7 @@ def tile_metalinearheadml_pb_k_kernel(tc, r, psi_w1, psi_b1, w_dw, b_dw, w_gate,
         tail_pool = stack.enter_context(tc.tile_pool(name="tail", bufs=E_SETS))
         banks = stack.enter_context(tc.psum_pool(name="banks", bufs=4))
         accs = stack.enter_context(tc.psum_pool(name="accs", bufs=1))
+        stack.enter_context(tc.manual_schedule())
 
         ident = consts.tile([P, P], F32)
         make_identity(nc, ident[:])
@@ -68,11 +69,15 @@ def tile_metalinearheadml_pb_k_kernel(tc, r, psi_w1, psi_b1, w_dw, b_dw, w_gate,
 
         def load_chunk(c):
             raw = raw_pool.tile([P, ROW_SETS, CHUNK_K], BF16)
-            k = slice(c * CHUNK_K, (c + 1) * CHUNK_K)
-            nc.sync.dma_start(out=raw[:, 0:CLASS_SETS, :], in_=r_rows[:, :, k])
-            for u in range(2):
-                first = CLASS_SETS + 2 * u
-                nc.sync.dma_start(out=raw[:, first : first + 2, :], in_=w1_rows[u][:, :, k])
+            pieces = CHUNK_PASSES if c == CHUNKS - 1 else 1
+            width = CHUNK_K // pieces
+            for piece in range(pieces):
+                cols = slice(piece * width, (piece + 1) * width)
+                k = slice(c * CHUNK_K + piece * width, c * CHUNK_K + (piece + 1) * width)
+                nc.sync.dma_start(out=raw[:, 0:CLASS_SETS, cols], in_=r_rows[:, :, k])
+                for u in range(2):
+                    first = CLASS_SETS + 2 * u
+                    nc.sync.dma_start(out=raw[:, first : first + 2, cols], in_=w1_rows[u][:, :, k])
             return raw
 
         raw_chunks = {}
@@ -141,7 +146,7 @@ def tile_metalinearheadml_pb_k_kernel(tc, r, psi_w1, psi_b1, w_dw, b_dw, w_gate,
 
         w2_codes = consts.tile([P, 2 * E_SETS * P], U32, align_bytes=64)
         w2_scales = consts.tile([P, 2 * E_SETS * P], U8, align_bytes=64)
-        w2_grouped_of = {}
+        w2_grouped = consts.tile([P, 2 * E_SETS, P, PACK], BF16, align_bytes=64)
         bias_cols = consts.tile([P, 16], F32)
         w0_all = consts.tile([P, E], F32)
 
@@ -156,21 +161,25 @@ def tile_metalinearheadml_pb_k_kernel(tc, r, psi_w1, psi_b1, w_dw, b_dw, w_gate,
                 )
                 nc.scalar.copy(out=w0_all[:, first : first + width], in_=w0_bank[:, 0:width])
 
-        def transpose_w2_pair(pair):
-            w2_grouped = grouped_pool.tile([P, 2, P, PACK], BF16, align_bytes=64)
-            transpose_pair(w2_raw[:].bitcast(F32)[:, 2 * pair : 2 * pair + 2, :], w2_grouped[:], nc.scalar.copy)
-            w2_grouped_of[pair] = w2_grouped
-
-        def quantise_w2_pair(pair):
-            cols = slice(2 * pair * P, (2 * pair + 2) * P)
-            nc.vector.quantize_mx(
-                out=w2_codes[:, cols].bitcast(FP8X4),
-                scales=w2_scales[:, cols],
-                in_=w2_grouped_of[pair][:].rearrange("p s m t -> p (s m t)"),
-            )
+        def prepare_second_stage():
+            w2_words = w2_raw[:].bitcast(F32)
+            for pair in range(E_SETS):
+                sets = slice(2 * pair, 2 * pair + 2)
+                copy = nc.vector.tensor_copy if pair % 3 == 0 else nc.scalar.copy
+                transpose_pair(w2_words[:, sets, :], w2_grouped[:, sets], copy)
+            flat = w2_grouped[:].rearrange("p s m t -> p (s m t)")
+            for first, sets in ((0, 8), (8, 4)):
+                cols = slice(first * P, (first + sets) * P)
+                nc.vector.quantize_mx(
+                    out=w2_codes[:, cols].bitcast(FP8X4),
+                    scales=w2_scales[:, cols],
+                    in_=flat[:, first * K_PASS : (first + sets) * K_PASS],
+                )
 
         for i in range(ROUNDS + 2):
             for g in range(i * RUN, (i + 1) * RUN):
+                if g == PREP_PASS:
+                    prepare_second_stage()
                 if g < PASSES:
                     transpose_pass(g)
                     last_of_chunk = g % CHUNK_PASSES == CHUNK_PASSES - 1
@@ -178,12 +187,8 @@ def tile_metalinearheadml_pb_k_kernel(tc, r, psi_w1, psi_b1, w_dw, b_dw, w_gate,
                         raw_chunks[g // CHUNK_PASSES + RAW_BUFS] = load_chunk(g // CHUNK_PASSES + RAW_BUFS)
                 if g == CHUNK_PASSES - 1:
                     spread_small_operands()
-                if 0 <= g - PREP_PASS < E_SETS:
-                    transpose_w2_pair(g - PREP_PASS)
                 if 0 <= g - RUN < PASSES:
                     quantise_pass(g - RUN)
-                if 0 <= g - RUN - PREP_PASS < E_SETS:
-                    quantise_w2_pair(g - RUN - PREP_PASS)
             for g in range((i - 2) * RUN, (i - 1) * RUN):
                 if 0 <= g:
                     multiply_pass(g)

from contextlib import ExitStack

import concourse.mybir as mybir
from concourse.masks import make_identity

F32 = mybir.dt.float32
BF16 = mybir.dt.bfloat16
U32 = mybir.dt.uint32
U8 = mybir.dt.uint8
FP8X4 = mybir.dt.float8_e4m3fn_x4
ACT = mybir.ActivationFunctionType
ALU = mybir.AluOpType

P = 128
PACK = 4
K_PASS = P * PACK
WORDS_PASS = K_PASS // 2

CLASSES, R, HD, E = 256, 16384, 512, 768
PASSES = R // K_PASS
CLASS_SETS = CLASSES // P
HD_SETS = HD // P
ROW_SETS = CLASS_SETS + HD_SETS
E_SETS = E // P
E_PAIRS = E_SETS // 2

CHUNK_PASSES = 2
CHUNK_K = CHUNK_PASSES * K_PASS
CHUNKS = PASSES // CHUNK_PASSES
RAW_BUFS = 8
RUN = 1
ROUNDS = PASSES // RUN
PREP_PASS = RAW_BUFS * CHUNK_PASSES

FLOPS = 2 * CLASSES * R * HD + 2 * 2 * CLASSES * HD * E


def tile_metalinearheadml_pb_k_kernel(tc, r, psi_w1, psi_b1, w_dw, b_dw, w_gate, b_gate, W0, out):
    nc = tc.nc
    with ExitStack() as stack:
        consts = stack.enter_context(tc.tile_pool(name="consts", bufs=1))
        raw_pool = stack.enter_context(tc.tile_pool(name="raw", bufs=RAW_BUFS))
        grouped_pool = stack.enter_context(tc.tile_pool(name="grouped", bufs=2 * RUN + 2))
        codes_pool = stack.enter_context(tc.tile_pool(name="codes", bufs=3 * RUN + 2))
        tail_pool = stack.enter_context(tc.tile_pool(name="tail", bufs=E_SETS))
        banks = stack.enter_context(tc.psum_pool(name="banks", bufs=4))
        accs = stack.enter_context(tc.psum_pool(name="accs", bufs=1))
        stack.enter_context(tc.manual_schedule())

        ident = consts.tile([P, P], F32)
        make_identity(nc, ident[:])
        ones = consts.tile([P, P], BF16)
        nc.vector.memset(ones[:], 1.0)

        bias_rows = consts.tile([P, 2 * P], BF16)
        nc.vector.memset(bias_rows[:], 0.0)
        nc.scalar.dma_start(out=bias_rows[0:2, :], in_=psi_b1.rearrange("(v c) -> v c", c=2 * P))
        nc.scalar.dma_start(out=bias_rows[2:5, :], in_=b_gate.rearrange("(v c) -> v c", c=2 * P))
        nc.scalar.dma_start(out=bias_rows[5:8, :], in_=b_dw.rearrange("(v c) -> v c", c=2 * P))
        w0_rows = consts.tile([P, E], BF16)
        nc.vector.memset(w0_rows[:], 0.0)
        nc.scalar.dma_start(out=w0_rows[0:1, :], in_=W0.rearrange("(o c) -> o c", o=1))
        warm = consts.tile([P, 2], F32)
        nc.vector.memset(warm[:], 0.0)
        nc.scalar.activation(out=warm[:, 1:2], in_=warm[:, 0:1], func=ACT.Sigmoid)

        r_rows = r.rearrange("(s p) k -> p s k", p=P)
        w1_rows = psi_w1.rearrange("(u p e) k -> u p e k", u=2, e=2)

        def load_chunk(c):
            raw = raw_pool.tile([P, ROW_SETS, CHUNK_K], BF16)
            pieces = CHUNK_PASSES if c == CHUNKS - 1 else 1
            width = CHUNK_K // pieces
            for piece in range(pieces):
                cols = slice(piece * width, (piece + 1) * width)
                k = slice(c * CHUNK_K + piece * width, c * CHUNK_K + (piece + 1) * width)
                nc.sync.dma_start(out=raw[:, 0:CLASS_SETS, cols], in_=r_rows[:, :, k])
                for u in range(2):
                    first = CLASS_SETS + 2 * u
                    nc.sync.dma_start(out=raw[:, first : first + 2, cols], in_=w1_rows[u][:, :, k])
            return raw

        raw_chunks = {}
        for c in range(RAW_BUFS):
            raw_chunks[c] = load_chunk(c)

        w2_raw = consts.tile([P, 2 * E_SETS, HD], BF16)
        nc.sync.dma_start(
            out=w2_raw[:, 0:E_SETS, :].rearrange("p (v e) k -> p v (e k)", e=2),
            in_=w_gate.rearrange("(v p e) k -> p v (e k)", p=P, e=2),
        )
        nc.sync.dma_start(
            out=w2_raw[:, E_SETS : 2 * E_SETS, :].rearrange("p (v e) k -> p v (e k)", e=2),
            in_=w_dw.rearrange("(v p e) k -> p v (e k)", p=P, e=2),
        )
        B1_COL, BGATE_COL, BDW_COL = 0, 4, 10

        def transpose_pair(words, grouped, copy):
            bank = banks.tile([P, 2, 2, P], F32, tag="bank")
            for s in range(2):
                for u in range(2):
                    nc.tensor.transpose(bank[:, s, u, :], words[:, s, u * P : (u + 1) * P], ident[:])
            copy(out=grouped.bitcast(F32), in_=bank[:].rearrange("p s u m -> p s m u"))

        hid_acc = [accs.tile([P, CLASSES], F32, name="acc%d" % t, tag="acc%d" % t) for t in range(HD_SETS)]
        grouped_of = {}
        codes_of = {}

        def transpose_pass(g):
            words = raw_chunks[g // CHUNK_PASSES][:].bitcast(F32)
            cols = slice((g % CHUNK_PASSES) * WORDS_PASS, (g % CHUNK_PASSES + 1) * WORDS_PASS)
            r_grouped = grouped_pool.tile([P, CLASS_SETS, P, PACK], BF16, align_bytes=64)
            w_grouped = grouped_pool.tile([P, HD_SETS, P, PACK], BF16, align_bytes=64)
            transpose_pair(words[:, 0:2, cols], r_grouped[:], nc.vector.tensor_copy)
            transpose_pair(words[:, 2:4, cols], w_grouped[:, 0:2], nc.scalar.copy)
            transpose_pair(words[:, 4:6, cols], w_grouped[:, 2:4], nc.scalar.copy)
            grouped_of[g] = (r_grouped, w_grouped)

        def quantise_pass(g):
            r_grouped, w_grouped = grouped_of[g]
            r_codes = codes_pool.tile([P, CLASSES], U32, align_bytes=64)
            r_scales = codes_pool.tile([P, CLASSES], U8, align_bytes=64)
            w_codes = codes_pool.tile([P, HD], U32, align_bytes=64)
            w_scales = codes_pool.tile([P, HD], U8, align_bytes=64)
            nc.vector.quantize_mx(
                out=r_codes[:].bitcast(FP8X4), scales=r_scales[:], in_=r_grouped[:].rearrange("p s m t -> p (s m t)")
            )
            nc.vector.quantize_mx(
                out=w_codes[:].bitcast(FP8X4), scales=w_scales[:], in_=w_grouped[:].rearrange("p s m t -> p (s m t)")
            )
            codes_of[g] = (r_codes, r_scales, w_codes, w_scales)

        def multiply_pass(g):
            r_codes, r_scales, w_codes, w_scales = codes_of[g]
            for t in range(HD_SETS):
                units = slice(t * P, (t + 1) * P)
                nc.tensor.matmul_mx(
                    out=hid_acc[t][:],
                    lhsT=w_codes[:, units].bitcast(FP8X4),
                    lhsT_scale=w_scales[:, units],
                    rhs=r_codes[:].bitcast(FP8X4),
                    rhs_scale=r_scales[:],
                    start=(g == 0),
                    stop=(g == PASSES - 1),
                )

        w2_codes = consts.tile([P, 2 * E_SETS * P], U32, align_bytes=64)
        w2_scales = consts.tile([P, 2 * E_SETS * P], U8, align_bytes=64)
        w2_grouped = consts.tile([P, 2 * E_SETS, P, PACK], BF16, align_bytes=64)
        bias_cols = consts.tile([P, 16], F32)
        w0_all = consts.tile([P, E], F32)

        def spread_small_operands():
            bias_bank = banks.tile([P, 4 * P], F32, tag="bank")
            nc.tensor.transpose(bias_bank[:, 0:P], bias_rows[:].bitcast(F32), ident[:])
            nc.vector.tensor_copy(out=bias_cols[:], in_=bias_bank[:, 0:8].bitcast(BF16))
            for first, width in ((0, 512), (512, 256)):
                w0_bank = banks.tile([P, 4 * P], F32, tag="bank")
                nc.tensor.matmul(
                    out=w0_bank[:, 0:width], lhsT=ones[:], rhs=w0_rows[:, first : first + width], start=True, stop=True
                )
                nc.scalar.copy(out=w0_all[:, first : first + width], in_=w0_bank[:, 0:width])

        def prepare_second_stage():
            w2_words = w2_raw[:].bitcast(F32)
            for pair in range(E_SETS):
                sets = slice(2 * pair, 2 * pair + 2)
                copy = nc.vector.tensor_copy if pair % 3 == 0 else nc.scalar.copy
                transpose_pair(w2_words[:, sets, :], w2_grouped[:, sets], copy)
            flat = w2_grouped[:].rearrange("p s m t -> p (s m t)")
            for first, sets in ((0, 8), (8, 4)):
                cols = slice(first * P, (first + sets) * P)
                nc.vector.quantize_mx(
                    out=w2_codes[:, cols].bitcast(FP8X4),
                    scales=w2_scales[:, cols],
                    in_=flat[:, first * K_PASS : (first + sets) * K_PASS],
                )

        for i in range(ROUNDS + 2):
            for g in range(i * RUN, (i + 1) * RUN):
                if g == PREP_PASS:
                    prepare_second_stage()
                if g < PASSES:
                    transpose_pass(g)
                    last_of_chunk = g % CHUNK_PASSES == CHUNK_PASSES - 1
                    if last_of_chunk and g // CHUNK_PASSES + RAW_BUFS < CHUNKS:
                        raw_chunks[g // CHUNK_PASSES + RAW_BUFS] = load_chunk(g // CHUNK_PASSES + RAW_BUFS)
                if g == CHUNK_PASSES - 1:
                    spread_small_operands()
                if 0 <= g - RUN < PASSES:
                    quantise_pass(g - RUN)
            for g in range((i - 2) * RUN, (i - 1) * RUN):
                if 0 <= g:
                    multiply_pass(g)

        hid_planes = consts.tile([P, HD_SETS, CLASSES], BF16)
        for t in range(HD_SETS):
            bias = bias_cols[:, B1_COL + t : B1_COL + t + 1]
            if t % 2 == 0:
                nc.scalar.activation(out=hid_planes[:, t, :], in_=hid_acc[t][:], func=ACT.Relu, bias=bias, scale=1.0)
            else:
                nc.vector.tensor_scalar(
                    out=hid_planes[:, t, :], in0=hid_acc[t][:], scalar1=bias, scalar2=0.0, op0=ALU.add, op1=ALU.max
                )
        hid_grouped = consts.tile([P, CLASSES, PACK], BF16, align_bytes=64)
        nc.vector.tensor_copy(out=hid_grouped[:], in_=hid_planes[:].rearrange("p t c -> p c t"))
        hid_codes = consts.tile([P, CLASSES], U32, align_bytes=64)
        hid_scales = consts.tile([P, CLASSES], U8, align_bytes=64)
        nc.vector.quantize_mx(
            out=hid_codes[:].bitcast(FP8X4), scales=hid_scales[:], in_=hid_grouped[:].rearrange("p c t -> p (c t)")
        )

        products = []
        for j in range(E_SETS):
            pre = banks.tile([P, 2, CLASSES], F32, tag="bank")
            for plane in range(2):
                outputs = slice((plane * E_SETS + j) * P, (plane * E_SETS + j + 1) * P)
                nc.tensor.matmul_mx(
                    out=pre[:, plane, :],
                    lhsT=w2_codes[:, outputs].bitcast(FP8X4),
                    lhsT_scale=w2_scales[:, outputs],
                    rhs=hid_codes[:].bitcast(FP8X4),
                    rhs_scale=hid_scales[:],
                    start=True,
                    stop=True,
                )
            gate = tail_pool.tile([P, CLASSES], F32)
            nc.scalar.activation(
                out=gate[:], in_=pre[:, 0, :], func=ACT.Sigmoid, bias=bias_cols[:, BGATE_COL + j : BGATE_COL + j + 1], scale=1.0
            )
            product = tail_pool.tile([P, CLASSES], F32)
            nc.vector.scalar_tensor_tensor(
                out=product[:],
                in0=pre[:, 1, :],
                scalar=bias_cols[:, BDW_COL + j : BDW_COL + j + 1],
                in1=gate[:],
                op0=ALU.add,
                op1=ALU.mult,
            )
            products.append(product)

        out_rows = out.rearrange("(c p) x -> p c x", p=P)
        for v in range(E_PAIRS):
            back = accs.tile([P, CLASS_SETS, 2, P], F32, name="back%d" % v, tag="acc%d" % v)
            for e in range(2):
                for c in range(CLASS_SETS):
                    nc.tensor.transpose(back[:, c, e, :], products[2 * v + e][:, c * P : (c + 1) * P], ident[:])
            result = tail_pool.tile([P, CLASS_SETS, 2 * P], F32, bufs=E_PAIRS)
            outputs = slice(v * 2 * P, (v + 1) * 2 * P)
            w0_pairs = w0_all[:, outputs].rearrange("p (m e) -> p m e", e=2)
            nc.vector.tensor_tensor(
                out=result[:].rearrange("p c (m e) -> p c m e", e=2),
                in0=back[:].rearrange("p c e m -> p c m e"),
                in1=w0_pairs.unsqueeze(1).to_broadcast([P, CLASS_SETS, P, 2]),
                op=ALU.add,
            )
            nc.sync.dma_start(out=out_rows[:, :, outputs], in_=result[:])
